import numpy as np
import ml_dtypes

BF16 = ml_dtypes.bfloat16


def bf(x):
    return np.asarray(x, np.float32).astype(BF16)


def f32(x):
    return np.asarray(x, np.float32)


def f64(x):
    return np.asarray(x).astype(np.float64)


def striped(idx):
    return np.tile(idx.reshape(-1, 16).T, (8, 1))


C, M, S, N = 128, 256, 512, 128


def sigmoid(v):
    return 1.0 / (1.0 + np.exp(-v))


def silu(v):
    return v * sigmoid(v)


def setup_inputs():
    return {
        "base": f32(np.random.standard_normal((C, S))),
        "h": bf(np.random.standard_normal((C, N))),
        "w_self": bf(0.25 * np.random.standard_normal((C, M)) / np.sqrt(C)),
        "w_nbr": bf(0.25 * np.random.standard_normal((C, M)) / np.sqrt(C)),
        "eb": f32(0.1 * np.random.standard_normal((M, 1))),
        "cond": f32(np.random.standard_normal((C, 1))),
        "offs": striped(np.random.permutation(S)[:N]),
    }


def reference(base, h, w_self, w_nbr, eb, cond, offs):
    idx = offs[:16].T.reshape(-1)
    p = f64(w_self).T @ f64(h) + f64(eb)
    q = f64(w_nbr).T @ f64(h)
    e = p[:, :, None] + q[:, None, :]
    msg = sigmoid(e[:C]) * silu(e[C:])
    agg = msg.sum(axis=2)
    out = f64(base).copy()
    out[:, idx] = (f64(h) + silu(f64(cond))) + agg
    return out

@@ -1,0 +1,88 @@
+import concourse.mybir as mybir
+
+F32 = mybir.dt.float32
+BF16 = mybir.dt.bfloat16
+U16 = mybir.dt.uint16
+ADD = mybir.AluOpType.add
+MULT = mybir.AluOpType.mult
+TANH = mybir.ActivationFunctionType.Tanh
+SILU = mybir.ActivationFunctionType.Silu
+
+C = 128
+N = 128
+S = 512
+JB = 4
+
+FLOPS = 2 * 2 * C * (2 * C) * N
+
+
+def tile_denoisingdecoder_kernel(tc, base, h, w_self, w_nbr, eb, cond, offs, out):
+    nc = tc.nc
+    with (
+        tc.tile_pool(name="held", bufs=1) as held,
+        tc.tile_pool(name="work", bufs=3) as work,
+        tc.psum_pool(name="psum", bufs=1) as psum,
+    ):
+        h_sb = held.tile([C, N], BF16)
+        w_nbr_sb = held.tile([C, 2 * C], BF16)
+        w_self_sb = held.tile([C, 2 * C], BF16)
+        eb_row = held.tile([1, 2 * C], F32)
+        cond_row = held.tile([1, C], F32)
+        offsets = held.tile([C, N // 16], U16)
+        window = held.tile([C, S], F32)
+        nc.sync.dma_start(h_sb[:], h)
+        nc.scalar.dma_start(w_nbr_sb[:], w_nbr)
+        nc.gpsimd.dma_start(w_self_sb[:], w_self)
+        nc.sync.dma_start(eb_row[:], eb.rearrange("m o -> o m"))
+        nc.gpsimd.dma_start(cond_row[:], cond.rearrange("c o -> o c"))
+        nc.sync.dma_start(offsets[:], offs)
+        nc.gpsimd.dma_start(window[:], base)
+
+        ones_row = held.tile([1, N], F32)
+        nc.vector.memset(ones_row[:], 1.0)
+
+        q_ps = [psum.tile([C, N], F32, name=f"q_ps{half}") for half in range(2)]
+        p_ps = [psum.tile([C, N], F32, name=f"p_ps{half}") for half in range(2)]
+        for half in range(2):
+            rows = slice(half * C, (half + 1) * C)
+            nc.tensor.matmul(q_ps[half][:], w_nbr_sb[:, rows], h_sb[:], start=True, stop=False)
+            nc.tensor.matmul(q_ps[half][:], eb_row[:, rows], ones_row[:], start=False, stop=True)
+            nc.tensor.matmul(p_ps[half][:], w_self_sb[:, rows], h_sb[:], start=True, stop=True)
+        cond_ps = psum.tile([C, 1], F32)
+        nc.tensor.matmul(cond_ps[:], cond_row[:], ones_row[:, 0:1], start=True, stop=True)
+
+        q_gate = held.tile([C, N], F32)
+        p_gate_half = held.tile([C, N], F32)
+        q_core = held.tile([C, N], F32)
+        p_core = held.tile([C, N], F32)
+        nc.vector.tensor_copy(q_gate[:], q_ps[0][:])
+        nc.vector.tensor_scalar_mul(p_gate_half[:], p_ps[0][:], 0.5)
+        nc.vector.tensor_copy(q_core[:], q_ps[1][:])
+        nc.vector.tensor_copy(p_core[:], p_ps[1][:])
+
+        silu_cond = held.tile([C, 1], F32)
+        nc.scalar.activation(silu_cond[:], cond_ps[:], SILU)
+        residual = held.tile([C, N], F32)
+        nc.vector.tensor_scalar_add(residual[:], h_sb[:], silu_cond[:])
+
+        twice_agg = held.tile([C, N], F32)
+        for block in range(N // JB):
+            tanh_gate = work.tile([C, JB, N], F32)
+            silu_core = work.tile([C, JB, N], F32)
+            for i in range(JB):
+                j = block * JB + i
+                nc.scalar.activation(
+                    tanh_gate[:, i, :], q_gate[:], TANH, bias=p_gate_half[:, j : j + 1], scale=0.5
+                )
+                nc.scalar.activation(silu_core[:, i, :], q_core[:], SILU, bias=p_core[:, j : j + 1])
+            message = work.tile([C, JB, N], F32)
+            nc.vector.scalar_tensor_tensor(message[:], tanh_gate[:], 1.0, silu_core[:], ADD, MULT)
+            nc.vector.tensor_reduce(
+                twice_agg[:, block * JB : (block + 1) * JB], message[:], mybir.AxisListType.X, ADD
+            )
+
+        agg = held.tile([C, N], F32)
+        nc.vector.tensor_scalar_mul(agg[:], twice_agg[:], 0.5)
+
+        nc.vector.tensor_tensor(window[:].indirect(offsets[:]), residual[:], agg[:], ADD)
+        nc.sync.dma_start(out, window[:])

@@ -11,7 +11,6 @@ SILU = mybir.ActivationFunctionType.Silu
 C = 128
 N = 128
 S = 512
-JB = 4
 
 FLOPS = 2 * 2 * C * (2 * C) * N
 
@@ -20,7 +19,7 @@ def tile_denoisingdecoder_kernel(tc, base, h, w_self, w_nbr, eb, cond, offs, out
     nc = tc.nc
     with (
         tc.tile_pool(name="held", bufs=1) as held,
-        tc.tile_pool(name="work", bufs=3) as work,
+        tc.tile_pool(name="work", bufs=6) as work,
         tc.psum_pool(name="psum", bufs=1) as psum,
     ):
         h_sb = held.tile([C, N], BF16)
@@ -66,19 +65,14 @@ def tile_denoisingdecoder_kernel(tc, base, h, w_self, w_nbr, eb, cond, offs, out
         nc.vector.tensor_scalar_add(residual[:], h_sb[:], silu_cond[:])
 
         twice_agg = held.tile([C, N], F32)
-        for block in range(N // JB):
-            tanh_gate = work.tile([C, JB, N], F32)
-            silu_core = work.tile([C, JB, N], F32)
-            for i in range(JB):
-                j = block * JB + i
-                nc.scalar.activation(
-                    tanh_gate[:, i, :], q_gate[:], TANH, bias=p_gate_half[:, j : j + 1], scale=0.5
-                )
-                nc.scalar.activation(silu_core[:, i, :], q_core[:], SILU, bias=p_core[:, j : j + 1])
-            message = work.tile([C, JB, N], F32)
-            nc.vector.scalar_tensor_tensor(message[:], tanh_gate[:], 1.0, silu_core[:], ADD, MULT)
-            nc.vector.tensor_reduce(
-                twice_agg[:, block * JB : (block + 1) * JB], message[:], mybir.AxisListType.X, ADD
+        for j in range(N):
+            tanh_gate = work.tile([C, N], F32)
+            silu_core = work.tile([C, N], F32)
+            nc.scalar.activation(tanh_gate[:], q_gate[:], TANH, bias=p_gate_half[:, j : j + 1], scale=0.5)
+            nc.scalar.activation(silu_core[:], q_core[:], SILU, bias=p_core[:, j : j + 1])
+            message = work.tile([C, N], F32)
+            nc.vector.scalar_tensor_tensor(
+                message[:], tanh_gate[:], 1.0, silu_core[:], ADD, MULT, accum_out=twice_agg[:, j : j + 1]
             )
 
         agg = held.tile([C, N], F32)

@@ -11,6 +11,7 @@ SILU = mybir.ActivationFunctionType.Silu
 C = 128
 N = 128
 S = 512
+JB = 4
 
 FLOPS = 2 * 2 * C * (2 * C) * N
 
@@ -19,61 +20,65 @@ def tile_denoisingdecoder_kernel(tc, base, h, w_self, w_nbr, eb, cond, offs, out
     nc = tc.nc
     with (
         tc.tile_pool(name="held", bufs=1) as held,
-        tc.tile_pool(name="work", bufs=6) as work,
-        tc.psum_pool(name="psum", bufs=1) as psum,
+        tc.tile_pool(name="work", bufs=3) as work,
+        tc.psum_pool(name="psum_cols", bufs=1) as psum_cols,
+        tc.psum_pool(name="psum_e", bufs=3) as psum_e,
     ):
         h_sb = held.tile([C, N], BF16)
-        w_nbr_sb = held.tile([C, 2 * C], BF16)
         w_self_sb = held.tile([C, 2 * C], BF16)
+        w_nbr_sb = held.tile([C, 2 * C], BF16)
         eb_row = held.tile([1, 2 * C], F32)
         cond_row = held.tile([1, C], F32)
         offsets = held.tile([C, N // 16], U16)
         window = held.tile([C, S], F32)
         nc.sync.dma_start(h_sb[:], h)
-        nc.scalar.dma_start(w_nbr_sb[:], w_nbr)
-        nc.gpsimd.dma_start(w_self_sb[:], w_self)
-        nc.sync.dma_start(eb_row[:], eb.rearrange("m o -> o m"))
+        nc.scalar.dma_start(w_self_sb[:], w_self)
+        nc.sync.dma_start(w_nbr_sb[:], w_nbr)
+        nc.scalar.dma_start(eb_row[:], eb.rearrange("m o -> o m"))
         nc.gpsimd.dma_start(cond_row[:], cond.rearrange("c o -> o c"))
         nc.sync.dma_start(offsets[:], offs)
         nc.gpsimd.dma_start(window[:], base)
 
-        ones_row = held.tile([1, N], F32)
-        nc.vector.memset(ones_row[:], 1.0)
-
-        q_ps = [psum.tile([C, N], F32, name=f"q_ps{half}") for half in range(2)]
-        p_ps = [psum.tile([C, N], F32, name=f"p_ps{half}") for half in range(2)]
-        for half in range(2):
-            rows = slice(half * C, (half + 1) * C)
-            nc.tensor.matmul(q_ps[half][:], w_nbr_sb[:, rows], h_sb[:], start=True, stop=False)
-            nc.tensor.matmul(q_ps[half][:], eb_row[:, rows], ones_row[:], start=False, stop=True)
-            nc.tensor.matmul(p_ps[half][:], w_self_sb[:, rows], h_sb[:], start=True, stop=True)
-        cond_ps = psum.tile([C, 1], F32)
-        nc.tensor.matmul(cond_ps[:], cond_row[:], ones_row[:, 0:1], start=True, stop=True)
-
-        q_gate = held.tile([C, N], F32)
-        p_gate_half = held.tile([C, N], F32)
-        q_core = held.tile([C, N], F32)
-        p_core = held.tile([C, N], F32)
-        nc.vector.tensor_copy(q_gate[:], q_ps[0][:])
-        nc.vector.tensor_scalar_mul(p_gate_half[:], p_ps[0][:], 0.5)
-        nc.vector.tensor_copy(q_core[:], q_ps[1][:])
-        nc.vector.tensor_copy(p_core[:], p_ps[1][:])
+        half_and_one = held.tile([1, 2], F32)
+        nc.vector.memset(half_and_one[:, 0:1], 0.5)
+        nc.vector.memset(half_and_one[:, 1:2], 1.0)
+        half = half_and_one[:, 0:1]
+        one = half_and_one[:, 1:2]
+        cols_ps = psum_cols.tile([C, 3], F32)
+        nc.tensor.matmul(cols_ps[:, 0:1], eb_row[:, 0:C], half, start=True, stop=True)
+        nc.tensor.matmul(cols_ps[:, 1:2], eb_row[:, C : 2 * C], one, start=True, stop=True)
+        nc.tensor.matmul(cols_ps[:, 2:3], cond_row[:], one, start=True, stop=True)
+        cols = held.tile([C, 3], F32)
+        nc.vector.tensor_copy(cols[:], cols_ps[:])
+        eb_gate_half = cols[:, 0:1]
+        eb_core = cols[:, 1:2]
 
         silu_cond = held.tile([C, 1], F32)
-        nc.scalar.activation(silu_cond[:], cond_ps[:], SILU)
+        nc.scalar.activation(silu_cond[:], cols[:, 2:3], SILU)
         residual = held.tile([C, N], F32)
         nc.vector.tensor_scalar_add(residual[:], h_sb[:], silu_cond[:])
 
         twice_agg = held.tile([C, N], F32)
-        for j in range(N):
-            tanh_gate = work.tile([C, N], F32)
-            silu_core = work.tile([C, N], F32)
-            nc.scalar.activation(tanh_gate[:], q_gate[:], TANH, bias=p_gate_half[:, j : j + 1], scale=0.5)
-            nc.scalar.activation(silu_core[:], q_core[:], SILU, bias=p_core[:, j : j + 1])
-            message = work.tile([C, N], F32)
-            nc.vector.scalar_tensor_tensor(
-                message[:], tanh_gate[:], 1.0, silu_core[:], ADD, MULT, accum_out=twice_agg[:, j : j + 1]
-            )
+        sending = h_sb[:].unsqueeze(1).to_broadcast([C, JB, N])
+        for block in range(N // JB):
+            j0 = block * JB
+            receiving = h_sb[:, j0 : j0 + JB].unsqueeze(2).to_broadcast([C, JB, N])
+            e_gate = psum_e.tile([C, JB, N], F32)
+            e_core = psum_e.tile([C, JB, N], F32)
+            nc.tensor.matmul(e_gate[:], w_self_sb[:, 0:C], receiving, start=True, stop=False)
+            nc.tensor.matmul(e_gate[:], w_nbr_sb[:, 0:C], sending, start=False, stop=True)
+            nc.tensor.matmul(e_core[:], w_self_sb[:, C : 2 * C], receiving, start=True, stop=False)
+            nc.tensor.matmul(e_core[:], w_nbr_sb[:, C : 2 * C], sending, start=False, stop=True)
+            tanh_gate = work.tile([C, JB, N], F32)
+            silu_core = work.tile([C, JB, N], F32)
+            nc.scalar.activation(tanh_gate[:], e_gate[:], TANH, bias=eb_gate_half, scale=0.5)
+            nc.scalar.activation(silu_core[:], e_core[:], SILU, bias=eb_core)
+            for i in range(JB):
+                message = work.tile([C, N], F32)
+                nc.vector.scalar_tensor_tensor(
+                    message[:], tanh_gate[:, i, :], 1.0, silu_core[:, i, :], ADD, MULT,
+                    accum_out=twice_agg[:, j0 + i : j0 + i + 1],
+                )
 
         agg = held.tile([C, N], F32)
         nc.vector.tensor_scalar_mul(agg[:], twice_agg[:], 0.5)

@@ -12,6 +12,7 @@ C = 128
 N = 128
 S = 512
 JB = 4
+WARM_UPS = 4
 
 FLOPS = 2 * 2 * C * (2 * C) * N
 
@@ -21,7 +22,7 @@ def tile_denoisingdecoder_kernel(tc, base, h, w_self, w_nbr, eb, cond, offs, out
     with (
         tc.tile_pool(name="held", bufs=1) as held,
         tc.tile_pool(name="work", bufs=3) as work,
-        tc.psum_pool(name="psum_cols", bufs=1) as psum_cols,
+        tc.psum_pool(name="psum_once", bufs=1) as psum_once,
         tc.psum_pool(name="psum_e", bufs=3) as psum_e,
     ):
         h_sb = held.tile([C, N], BF16)
@@ -39,12 +40,18 @@ def tile_denoisingdecoder_kernel(tc, base, h, w_self, w_nbr, eb, cond, offs, out
         nc.sync.dma_start(offsets[:], offs)
         nc.gpsimd.dma_start(window[:], base)
 
+        zeros = held.tile([C, JB * N], BF16)
+        nc.vector.memset(zeros[:], 0.0)
+        idle_ps = psum_once.tile([C, JB * N], F32)
+        for warm_up in range(WARM_UPS):
+            nc.tensor.matmul(idle_ps[:], zeros[:, 0:C], zeros[:], start=True, stop=True)
+
         half_and_one = held.tile([1, 2], F32)
         nc.vector.memset(half_and_one[:, 0:1], 0.5)
         nc.vector.memset(half_and_one[:, 1:2], 1.0)
         half = half_and_one[:, 0:1]
         one = half_and_one[:, 1:2]
-        cols_ps = psum_cols.tile([C, 3], F32)
+        cols_ps = psum_once.tile([C, 3], F32)
         nc.tensor.matmul(cols_ps[:, 0:1], eb_row[:, 0:C], half, start=True, stop=True)
         nc.tensor.matmul(cols_ps[:, 1:2], eb_row[:, C : 2 * C], one, start=True, stop=True)
         nc.tensor.matmul(cols_ps[:, 2:3], cond_row[:], one, start=True, stop=True)

@@ -12,7 +12,6 @@ C = 128
 N = 128
 S = 512
 JB = 4
-WARM_UPS = 4
 
 FLOPS = 2 * 2 * C * (2 * C) * N
 
@@ -22,7 +21,7 @@ def tile_denoisingdecoder_kernel(tc, base, h, w_self, w_nbr, eb, cond, offs, out
     with (
         tc.tile_pool(name="held", bufs=1) as held,
         tc.tile_pool(name="work", bufs=3) as work,
-        tc.psum_pool(name="psum_once", bufs=1) as psum_once,
+        tc.psum_pool(name="psum_cols", bufs=1) as psum_cols,
         tc.psum_pool(name="psum_e", bufs=3) as psum_e,
     ):
         h_sb = held.tile([C, N], BF16)
@@ -40,18 +39,12 @@ def tile_denoisingdecoder_kernel(tc, base, h, w_self, w_nbr, eb, cond, offs, out
         nc.sync.dma_start(offsets[:], offs)
         nc.gpsimd.dma_start(window[:], base)
 
-        zeros = held.tile([C, JB * N], BF16)
-        nc.vector.memset(zeros[:], 0.0)
-        idle_ps = psum_once.tile([C, JB * N], F32)
-        for warm_up in range(WARM_UPS):
-            nc.tensor.matmul(idle_ps[:], zeros[:, 0:C], zeros[:], start=True, stop=True)
-
         half_and_one = held.tile([1, 2], F32)
         nc.vector.memset(half_and_one[:, 0:1], 0.5)
         nc.vector.memset(half_and_one[:, 1:2], 1.0)
         half = half_and_one[:, 0:1]
         one = half_and_one[:, 1:2]
-        cols_ps = psum_once.tile([C, 3], F32)
+        cols_ps = psum_cols.tile([C, 3], F32)
         nc.tensor.matmul(cols_ps[:, 0:1], eb_row[:, 0:C], half, start=True, stop=True)
         nc.tensor.matmul(cols_ps[:, 1:2], eb_row[:, C : 2 * C], one, start=True, stop=True)
         nc.tensor.matmul(cols_ps[:, 2:3], cond_row[:], one, start=True, stop=True)
@@ -80,12 +73,9 @@ def tile_denoisingdecoder_kernel(tc, base, h, w_self, w_nbr, eb, cond, offs, out
             silu_core = work.tile([C, JB, N], F32)
             nc.scalar.activation(tanh_gate[:], e_gate[:], TANH, bias=eb_gate_half, scale=0.5)
             nc.scalar.activation(silu_core[:], e_core[:], SILU, bias=eb_core)
-            for i in range(JB):
-                message = work.tile([C, N], F32)
-                nc.vector.scalar_tensor_tensor(
-                    message[:], tanh_gate[:, i, :], 1.0, silu_core[:, i, :], ADD, MULT,
-                    accum_out=twice_agg[:, j0 + i : j0 + i + 1],
-                )
+            message = work.tile([C, JB, N], F32)
+            nc.vector.scalar_tensor_tensor(message[:], tanh_gate[:], 1.0, silu_core[:], ADD, MULT)
+            nc.vector.tensor_reduce(twice_agg[:, j0 : j0 + JB], message[:], mybir.AxisListType.X, ADD)
 
         agg = held.tile([C, N], F32)
         nc.vector.tensor_scalar_mul(agg[:], twice_agg[:], 0.5)

@@ -21,40 +21,30 @@ def tile_denoisingdecoder_kernel(tc, base, h, w_self, w_nbr, eb, cond, offs, out
     with (
         tc.tile_pool(name="held", bufs=1) as held,
         tc.tile_pool(name="work", bufs=3) as work,
-        tc.psum_pool(name="psum_cols", bufs=1) as psum_cols,
-        tc.psum_pool(name="psum_e", bufs=3) as psum_e,
+        tc.psum_pool(name="psum_e", bufs=4) as psum_e,
     ):
         h_sb = held.tile([C, N], BF16)
         w_self_sb = held.tile([C, 2 * C], BF16)
         w_nbr_sb = held.tile([C, 2 * C], BF16)
-        eb_row = held.tile([1, 2 * C], F32)
-        cond_row = held.tile([1, C], F32)
+        eb_gate = held.tile([C, 1], F32)
+        eb_core = held.tile([C, 1], F32)
+        cond_sb = held.tile([C, 1], F32)
         offsets = held.tile([C, N // 16], U16)
         window = held.tile([C, S], F32)
         nc.sync.dma_start(h_sb[:], h)
-        nc.scalar.dma_start(w_self_sb[:], w_self)
+        nc.scalar.dma_start(eb_gate[:], eb[0:C, :])
         nc.sync.dma_start(w_nbr_sb[:], w_nbr)
-        nc.scalar.dma_start(eb_row[:], eb.rearrange("m o -> o m"))
-        nc.gpsimd.dma_start(cond_row[:], cond.rearrange("c o -> o c"))
+        nc.scalar.dma_start(w_self_sb[:], w_self)
+        nc.sync.dma_start(eb_core[:], eb[C : 2 * C, :])
+        nc.scalar.dma_start(cond_sb[:], cond)
         nc.sync.dma_start(offsets[:], offs)
         nc.gpsimd.dma_start(window[:], base)
 
-        half_and_one = held.tile([1, 2], F32)
-        nc.vector.memset(half_and_one[:, 0:1], 0.5)
-        nc.vector.memset(half_and_one[:, 1:2], 1.0)
-        half = half_and_one[:, 0:1]
-        one = half_and_one[:, 1:2]
-        cols_ps = psum_cols.tile([C, 3], F32)
-        nc.tensor.matmul(cols_ps[:, 0:1], eb_row[:, 0:C], half, start=True, stop=True)
-        nc.tensor.matmul(cols_ps[:, 1:2], eb_row[:, C : 2 * C], one, start=True, stop=True)
-        nc.tensor.matmul(cols_ps[:, 2:3], cond_row[:], one, start=True, stop=True)
-        cols = held.tile([C, 3], F32)
-        nc.vector.tensor_copy(cols[:], cols_ps[:])
-        eb_gate_half = cols[:, 0:1]
-        eb_core = cols[:, 1:2]
+        eb_gate_half = held.tile([C, 1], F32)
+        nc.vector.tensor_scalar_mul(eb_gate_half[:], eb_gate[:], 0.5)
 
         silu_cond = held.tile([C, 1], F32)
-        nc.scalar.activation(silu_cond[:], cols[:, 2:3], SILU)
+        nc.scalar.activation(silu_cond[:], cond_sb[:], SILU)
         residual = held.tile([C, N], F32)
         nc.vector.tensor_scalar_add(residual[:], h_sb[:], silu_cond[:])
 
@@ -71,11 +61,14 @@ def tile_denoisingdecoder_kernel(tc, base, h, w_self, w_nbr, eb, cond, offs, out
             nc.tensor.matmul(e_core[:], w_nbr_sb[:, C : 2 * C], sending, start=False, stop=True)
             tanh_gate = work.tile([C, JB, N], F32)
             silu_core = work.tile([C, JB, N], F32)
-            nc.scalar.activation(tanh_gate[:], e_gate[:], TANH, bias=eb_gate_half, scale=0.5)
-            nc.scalar.activation(silu_core[:], e_core[:], SILU, bias=eb_core)
-            message = work.tile([C, JB, N], F32)
-            nc.vector.scalar_tensor_tensor(message[:], tanh_gate[:], 1.0, silu_core[:], ADD, MULT)
-            nc.vector.tensor_reduce(twice_agg[:, j0 : j0 + JB], message[:], mybir.AxisListType.X, ADD)
+            nc.scalar.activation(tanh_gate[:], e_gate[:], TANH, bias=eb_gate_half[:], scale=0.5)
+            nc.scalar.activation(silu_core[:], e_core[:], SILU, bias=eb_core[:])
+            for i in range(JB):
+                message = work.tile([C, N], F32)
+                nc.vector.scalar_tensor_tensor(
+                    message[:], tanh_gate[:, i, :], 1.0, silu_core[:, i, :], ADD, MULT,
+                    accum_out=twice_agg[:, j0 + i : j0 + i + 1],
+                )
 
         agg = held.tile([C, N], F32)
         nc.vector.tensor_scalar_mul(agg[:], twice_agg[:], 0.5)

@@ -32,11 +32,11 @@ def tile_denoisingdecoder_kernel(tc, base, h, w_self, w_nbr, eb, cond, offs, out
         offsets = held.tile([C, N // 16], U16)
         window = held.tile([C, S], F32)
         nc.sync.dma_start(h_sb[:], h)
-        nc.scalar.dma_start(eb_gate[:], eb[0:C, :])
-        nc.sync.dma_start(w_nbr_sb[:], w_nbr)
         nc.scalar.dma_start(w_self_sb[:], w_self)
-        nc.sync.dma_start(eb_core[:], eb[C : 2 * C, :])
+        nc.sync.dma_start(w_nbr_sb[:], w_nbr)
         nc.scalar.dma_start(cond_sb[:], cond)
+        nc.sync.dma_start(eb_gate[:], eb[0:C, :])
+        nc.sync.dma_start(eb_core[:], eb[C : 2 * C, :])
         nc.sync.dma_start(offsets[:], offs)
         nc.gpsimd.dma_start(window[:], base)
 

@@ -31,9 +31,9 @@ def tile_denoisingdecoder_kernel(tc, base, h, w_self, w_nbr, eb, cond, offs, out
         cond_sb = held.tile([C, 1], F32)
         offsets = held.tile([C, N // 16], U16)
         window = held.tile([C, S], F32)
-        nc.sync.dma_start(h_sb[:], h)
-        nc.scalar.dma_start(w_self_sb[:], w_self)
         nc.sync.dma_start(w_nbr_sb[:], w_nbr)
+        nc.scalar.dma_start(w_self_sb[:], w_self)
+        nc.sync.dma_start(h_sb[:], h)
         nc.scalar.dma_start(cond_sb[:], cond)
         nc.sync.dma_start(eb_gate[:], eb[0:C, :])
         nc.sync.dma_start(eb_core[:], eb[C : 2 * C, :])
@@ -48,21 +48,42 @@ def tile_denoisingdecoder_kernel(tc, base, h, w_self, w_nbr, eb, cond, offs, out
         residual = held.tile([C, N], F32)
         nc.vector.tensor_scalar_add(residual[:], h_sb[:], silu_cond[:])
 
+        qp_gate = psum_e.tile([C, N + JB], F32, tag="e_gate", name="qp_gate")
+        qp_core = psum_e.tile([C, N + JB], F32, tag="e_core", name="qp_core")
+        p_eb = held.tile([C, 2, JB], F32)
+        first_e = held.tile([C, 2, JB, N], F32)
+        for half, (qp, bias) in enumerate(((qp_gate, eb_gate), (qp_core, eb_core))):
+            q, p = qp[:, 0:N], qp[:, N : N + JB]
+            rows = slice(half * C, (half + 1) * C)
+            nc.tensor.matmul(q, w_nbr_sb[:, rows], h_sb[:], start=True, stop=True)
+            nc.tensor.matmul(p, w_self_sb[:, rows], h_sb[:, 0:JB], start=True, stop=True)
+            nc.vector.tensor_scalar_add(p_eb[:, half], p, bias[:])
+            nc.vector.tensor_tensor(
+                first_e[:, half],
+                q.unsqueeze(1).to_broadcast([C, JB, N]),
+                p_eb[:, half].unsqueeze(2).to_broadcast([C, JB, N]),
+                ADD,
+            )
+
         twice_agg = held.tile([C, N], F32)
         sending = h_sb[:].unsqueeze(1).to_broadcast([C, JB, N])
         for block in range(N // JB):
             j0 = block * JB
-            receiving = h_sb[:, j0 : j0 + JB].unsqueeze(2).to_broadcast([C, JB, N])
-            e_gate = psum_e.tile([C, JB, N], F32)
-            e_core = psum_e.tile([C, JB, N], F32)
-            nc.tensor.matmul(e_gate[:], w_self_sb[:, 0:C], receiving, start=True, stop=False)
-            nc.tensor.matmul(e_gate[:], w_nbr_sb[:, 0:C], sending, start=False, stop=True)
-            nc.tensor.matmul(e_core[:], w_self_sb[:, C : 2 * C], receiving, start=True, stop=False)
-            nc.tensor.matmul(e_core[:], w_nbr_sb[:, C : 2 * C], sending, start=False, stop=True)
             tanh_gate = work.tile([C, JB, N], F32)
             silu_core = work.tile([C, JB, N], F32)
-            nc.scalar.activation(tanh_gate[:], e_gate[:], TANH, bias=eb_gate_half[:], scale=0.5)
-            nc.scalar.activation(silu_core[:], e_core[:], SILU, bias=eb_core[:])
+            if block == 0:
+                nc.scalar.activation(tanh_gate[:], first_e[:, 0], TANH, scale=0.5)
+                nc.scalar.activation(silu_core[:], first_e[:, 1], SILU)
+            else:
+                receiving = h_sb[:, j0 : j0 + JB].unsqueeze(2).to_broadcast([C, JB, N])
+                e_gate = psum_e.tile([C, JB, N], F32)
+                e_core = psum_e.tile([C, JB, N], F32)
+                nc.tensor.matmul(e_gate[:], w_self_sb[:, 0:C], receiving, start=True, stop=False)
+                nc.tensor.matmul(e_gate[:], w_nbr_sb[:, 0:C], sending, start=False, stop=True)
+                nc.tensor.matmul(e_core[:], w_self_sb[:, C : 2 * C], receiving, start=True, stop=False)
+                nc.tensor.matmul(e_core[:], w_nbr_sb[:, C : 2 * C], sending, start=False, stop=True)
+                nc.scalar.activation(tanh_gate[:], e_gate[:], TANH, bias=eb_gate_half[:], scale=0.5)
+                nc.scalar.activation(silu_core[:], e_core[:], SILU, bias=eb_core[:])
             for i in range(JB):
                 message = work.tile([C, N], F32)
                 nc.vector.scalar_tensor_tensor(

@@ -13,6 +13,9 @@ N = 128
 S = 512
 JB = 4
 
+HALF = JB // 2
+BLOCKS = [HALF] * 2 + [JB] * (N // JB - 2) + [HALF] * 2
+
 FLOPS = 2 * 2 * C * (2 * C) * N
 
 
@@ -20,7 +23,7 @@ def tile_denoisingdecoder_kernel(tc, base, h, w_self, w_nbr, eb, cond, offs, out
     nc = tc.nc
     with (
         tc.tile_pool(name="held", bufs=1) as held,
-        tc.tile_pool(name="work", bufs=3) as work,
+        tc.tile_pool(name="work", bufs=4) as work,
         tc.psum_pool(name="psum_e", bufs=4) as psum_e,
     ):
         h_sb = held.tile([C, N], BF16)
@@ -58,38 +61,46 @@ def tile_denoisingdecoder_kernel(tc, base, h, w_self, w_nbr, eb, cond, offs, out
             nc.tensor.matmul(q, w_nbr_sb[:, rows], h_sb[:], start=True, stop=True)
             nc.tensor.matmul(p, w_self_sb[:, rows], h_sb[:, 0:JB], start=True, stop=True)
             nc.vector.tensor_scalar_add(p_eb[:, half], p, bias[:])
-            nc.vector.tensor_tensor(
-                first_e[:, half],
-                q.unsqueeze(1).to_broadcast([C, JB, N]),
-                p_eb[:, half].unsqueeze(2).to_broadcast([C, JB, N]),
-                ADD,
-            )
+
+        for j0 in (0, HALF):
+            for half, qp in enumerate((qp_gate, qp_core)):
+                nc.vector.tensor_tensor(
+                    first_e[:, half, j0 : j0 + HALF],
+                    qp[:, 0:N].unsqueeze(1).to_broadcast([C, HALF, N]),
+                    p_eb[:, half, j0 : j0 + HALF].unsqueeze(2).to_broadcast([C, HALF, N]),
+                    ADD,
+                )
 
         twice_agg = held.tile([C, N], F32)
-        sending = h_sb[:].unsqueeze(1).to_broadcast([C, JB, N])
-        for block in range(N // JB):
-            j0 = block * JB
+        j0 = 0
+        for width in BLOCKS:
             tanh_gate = work.tile([C, JB, N], F32)
             silu_core = work.tile([C, JB, N], F32)
-            if block == 0:
-                nc.scalar.activation(tanh_gate[:], first_e[:, 0], TANH, scale=0.5)
-                nc.scalar.activation(silu_core[:], first_e[:, 1], SILU)
+            if j0 < JB:
+                atoms = slice(j0, j0 + width)
+                nc.scalar.activation(tanh_gate[:, 0:width], first_e[:, 0, atoms], TANH, scale=0.5)
+                nc.scalar.activation(silu_core[:, 0:width], first_e[:, 1, atoms], SILU)
             else:
-                receiving = h_sb[:, j0 : j0 + JB].unsqueeze(2).to_broadcast([C, JB, N])
-                e_gate = psum_e.tile([C, JB, N], F32)
-                e_core = psum_e.tile([C, JB, N], F32)
-                nc.tensor.matmul(e_gate[:], w_self_sb[:, 0:C], receiving, start=True, stop=False)
-                nc.tensor.matmul(e_gate[:], w_nbr_sb[:, 0:C], sending, start=False, stop=True)
-                nc.tensor.matmul(e_core[:], w_self_sb[:, C : 2 * C], receiving, start=True, stop=False)
-                nc.tensor.matmul(e_core[:], w_nbr_sb[:, C : 2 * C], sending, start=False, stop=True)
-                nc.scalar.activation(tanh_gate[:], e_gate[:], TANH, bias=eb_gate_half[:], scale=0.5)
-                nc.scalar.activation(silu_core[:], e_core[:], SILU, bias=eb_core[:])
-            for i in range(JB):
+                sending = h_sb[:].unsqueeze(1).to_broadcast([C, width, N])
+                receiving = h_sb[:, j0 : j0 + width].unsqueeze(2).to_broadcast([C, width, N])
+                gate_tile = psum_e.tile([C, JB, N], F32, tag="e_gate", name="gate_tile")
+                core_tile = psum_e.tile([C, JB, N], F32, tag="e_core", name="core_tile")
+                e_gate, e_core = gate_tile[:, 0:width], core_tile[:, 0:width]
+                nc.tensor.matmul(e_gate, w_self_sb[:, 0:C], receiving, start=True, stop=False)
+                nc.tensor.matmul(e_gate, w_nbr_sb[:, 0:C], sending, start=False, stop=True)
+                nc.tensor.matmul(e_core, w_self_sb[:, C : 2 * C], receiving, start=True, stop=False)
+                nc.tensor.matmul(e_core, w_nbr_sb[:, C : 2 * C], sending, start=False, stop=True)
+                nc.scalar.activation(
+                    tanh_gate[:, 0:width], e_gate, TANH, bias=eb_gate_half[:], scale=0.5
+                )
+                nc.scalar.activation(silu_core[:, 0:width], e_core, SILU, bias=eb_core[:])
+            for i in range(width):
                 message = work.tile([C, N], F32)
                 nc.vector.scalar_tensor_tensor(
                     message[:], tanh_gate[:, i, :], 1.0, silu_core[:, i, :], ADD, MULT,
                     accum_out=twice_agg[:, j0 + i : j0 + i + 1],
                 )
+            j0 += width
 
         agg = held.tile([C, N], F32)
         nc.vector.tensor_scalar_mul(agg[:], twice_agg[:], 0.5)

@@ -13,8 +13,7 @@ N = 128
 S = 512
 JB = 4
 
-HALF = JB // 2
-BLOCKS = [HALF] * 2 + [JB] * (N // JB - 2) + [HALF] * 2
+BLOCKS = [JB] * (N // JB - 1) + [JB // 2] * 2
 
 FLOPS = 2 * 2 * C * (2 * C) * N
 
@@ -37,11 +36,16 @@ def tile_denoisingdecoder_kernel(tc, base, h, w_self, w_nbr, eb, cond, offs, out
         nc.sync.dma_start(w_nbr_sb[:], w_nbr)
         nc.scalar.dma_start(w_self_sb[:], w_self)
         nc.sync.dma_start(h_sb[:], h)
-        nc.scalar.dma_start(cond_sb[:], cond)
+        nc.scalar.dma_start(eb_core[:], eb[C : 2 * C, :])
         nc.sync.dma_start(eb_gate[:], eb[0:C, :])
-        nc.sync.dma_start(eb_core[:], eb[C : 2 * C, :])
+        nc.scalar.dma_start(cond_sb[:], cond)
         nc.sync.dma_start(offsets[:], offs)
         nc.gpsimd.dma_start(window[:], base)
+
+        zero = held.tile([C, 1], F32)
+        silu_zero = held.tile([C, 1], F32)
+        nc.vector.memset(zero[:], 0.0)
+        nc.scalar.activation(silu_zero[:], zero[:], SILU)
 
         eb_gate_half = held.tile([C, 1], F32)
         nc.vector.tensor_scalar_mul(eb_gate_half[:], eb_gate[:], 0.5)
@@ -51,35 +55,31 @@ def tile_denoisingdecoder_kernel(tc, base, h, w_self, w_nbr, eb, cond, offs, out
         residual = held.tile([C, N], F32)
         nc.vector.tensor_scalar_add(residual[:], h_sb[:], silu_cond[:])
 
-        qp_gate = psum_e.tile([C, N + JB], F32, tag="e_gate", name="qp_gate")
-        qp_core = psum_e.tile([C, N + JB], F32, tag="e_core", name="qp_core")
-        p_eb = held.tile([C, 2, JB], F32)
-        first_e = held.tile([C, 2, JB, N], F32)
-        for half, (qp, bias) in enumerate(((qp_gate, eb_gate), (qp_core, eb_core))):
-            q, p = qp[:, 0:N], qp[:, N : N + JB]
-            rows = slice(half * C, (half + 1) * C)
-            nc.tensor.matmul(q, w_nbr_sb[:, rows], h_sb[:], start=True, stop=True)
-            nc.tensor.matmul(p, w_self_sb[:, rows], h_sb[:, 0:JB], start=True, stop=True)
-            nc.vector.tensor_scalar_add(p_eb[:, half], p, bias[:])
-
-        for j0 in (0, HALF):
-            for half, qp in enumerate((qp_gate, qp_core)):
-                nc.vector.tensor_tensor(
-                    first_e[:, half, j0 : j0 + HALF],
-                    qp[:, 0:N].unsqueeze(1).to_broadcast([C, HALF, N]),
-                    p_eb[:, half, j0 : j0 + HALF].unsqueeze(2).to_broadcast([C, HALF, N]),
-                    ADD,
-                )
+        p = psum_e.tile([C, 2, JB], F32, tag="e_core", name="p")
+        q_gate = psum_e.tile([C, N], F32, tag="e_gate", name="q_gate")
+        q_core = psum_e.tile([C, N], F32, tag="e_core", name="q_core")
+        nc.tensor.matmul(p[:, 0], w_self_sb[:, 0:C], h_sb[:, 0:JB], start=True, stop=True)
+        nc.tensor.matmul(p[:, 1], w_self_sb[:, C : 2 * C], h_sb[:, 0:JB], start=True, stop=True)
+        nc.tensor.matmul(q_gate[:], w_nbr_sb[:, 0:C], h_sb[:], start=True, stop=True)
+        nc.tensor.matmul(q_core[:], w_nbr_sb[:, C : 2 * C], h_sb[:], start=True, stop=True)
+        p_gate_half = held.tile([C, JB], F32)
+        p_core = held.tile([C, JB], F32)
+        nc.vector.tensor_scalar(p_gate_half[:], p[:, 0], eb_gate[:], 0.5, ADD, MULT)
+        nc.vector.tensor_scalar_add(p_core[:], p[:, 1], eb_core[:])
 
         twice_agg = held.tile([C, N], F32)
         j0 = 0
         for width in BLOCKS:
             tanh_gate = work.tile([C, JB, N], F32)
             silu_core = work.tile([C, JB, N], F32)
-            if j0 < JB:
-                atoms = slice(j0, j0 + width)
-                nc.scalar.activation(tanh_gate[:, 0:width], first_e[:, 0, atoms], TANH, scale=0.5)
-                nc.scalar.activation(silu_core[:, 0:width], first_e[:, 1, atoms], SILU)
+            if j0 == 0:
+                for j in range(width):
+                    nc.scalar.activation(
+                        tanh_gate[:, j], q_gate[:], TANH, bias=p_gate_half[:, j : j + 1], scale=0.5
+                    )
+                    nc.scalar.activation(
+                        silu_core[:, j], q_core[:], SILU, bias=p_core[:, j : j + 1]
+                    )
             else:
                 sending = h_sb[:].unsqueeze(1).to_broadcast([C, width, N])
                 receiving = h_sb[:, j0 : j0 + width].unsqueeze(2).to_broadcast([C, width, N])

@@ -13,7 +13,7 @@ N = 128
 S = 512
 JB = 4
 
-BLOCKS = [JB] * (N // JB - 1) + [JB // 2] * 2
+BLOCKS = [JB] * (N // JB - 1) + [JB // 2, JB // 4, JB // 4]
 
 FLOPS = 2 * 2 * C * (2 * C) * N
 
@@ -55,19 +55,39 @@ def tile_denoisingdecoder_kernel(tc, base, h, w_self, w_nbr, eb, cond, offs, out
         residual = held.tile([C, N], F32)
         nc.vector.tensor_scalar_add(residual[:], h_sb[:], silu_cond[:])
 
-        p = psum_e.tile([C, 2, JB], F32, tag="e_core", name="p")
+        p = psum_e.tile([C, 2, 2 * JB], F32, tag="e_core", name="p")
         q_gate = psum_e.tile([C, N], F32, tag="e_gate", name="q_gate")
         q_core = psum_e.tile([C, N], F32, tag="e_core", name="q_core")
-        nc.tensor.matmul(p[:, 0], w_self_sb[:, 0:C], h_sb[:, 0:JB], start=True, stop=True)
-        nc.tensor.matmul(p[:, 1], w_self_sb[:, C : 2 * C], h_sb[:, 0:JB], start=True, stop=True)
+        early = h_sb[:, 0 : 2 * JB]
+        nc.tensor.matmul(p[:, 0], w_self_sb[:, 0:C], early, start=True, stop=True)
+        nc.tensor.matmul(p[:, 1], w_self_sb[:, C : 2 * C], early, start=True, stop=True)
         nc.tensor.matmul(q_gate[:], w_nbr_sb[:, 0:C], h_sb[:], start=True, stop=True)
         nc.tensor.matmul(q_core[:], w_nbr_sb[:, C : 2 * C], h_sb[:], start=True, stop=True)
-        p_gate_half = held.tile([C, JB], F32)
-        p_core = held.tile([C, JB], F32)
+        q_gate_vector = psum_e.tile([C, N], F32, tag="e_gate", name="q_gate_vector")
+        q_core_vector = psum_e.tile([C, N], F32, tag="e_core", name="q_core_vector")
+        nc.tensor.matmul(q_gate_vector[:], w_nbr_sb[:, 0:C], h_sb[:], start=True, stop=True)
+        nc.tensor.matmul(q_core_vector[:], w_nbr_sb[:, C : 2 * C], h_sb[:], start=True, stop=True)
+        p_gate_half = held.tile([C, 2 * JB], F32)
+        p_core = held.tile([C, 2 * JB], F32)
         nc.vector.tensor_scalar(p_gate_half[:], p[:, 0], eb_gate[:], 0.5, ADD, MULT)
         nc.vector.tensor_scalar_add(p_core[:], p[:, 1], eb_core[:])
+        half_e_gate = held.tile([C, JB, N], F32)
+        sbuf_e_core = held.tile([C, JB, N], F32)
+        for e, q, scale, p_eb in (
+            (half_e_gate, q_gate_vector, 0.5, p_gate_half),
+            (sbuf_e_core, q_core_vector, 1.0, p_core),
+        ):
+            nc.vector.scalar_tensor_tensor(
+                e[:],
+                q[:].unsqueeze(1).to_broadcast([C, JB, N]),
+                scale,
+                p_eb[:, JB : 2 * JB].unsqueeze(2).to_broadcast([C, JB, N]),
+                MULT,
+                ADD,
+            )
 
         twice_agg = held.tile([C, N], F32)
+        agg = held.tile([C, N], F32)
         j0 = 0
         for width in BLOCKS:
             tanh_gate = work.tile([C, JB, N], F32)
@@ -80,6 +100,9 @@ def tile_denoisingdecoder_kernel(tc, base, h, w_self, w_nbr, eb, cond, offs, out
                     nc.scalar.activation(
                         silu_core[:, j], q_core[:], SILU, bias=p_core[:, j : j + 1]
                     )
+            elif j0 == JB:
+                nc.scalar.activation(tanh_gate[:], half_e_gate[:], TANH)
+                nc.scalar.activation(silu_core[:], sbuf_e_core[:], SILU)
             else:
                 sending = h_sb[:].unsqueeze(1).to_broadcast([C, width, N])
                 receiving = h_sb[:, j0 : j0 + width].unsqueeze(2).to_broadcast([C, width, N])
@@ -94,16 +117,23 @@ def tile_denoisingdecoder_kernel(tc, base, h, w_self, w_nbr, eb, cond, offs, out
                     tanh_gate[:, 0:width], e_gate, TANH, bias=eb_gate_half[:], scale=0.5
                 )
                 nc.scalar.activation(silu_core[:, 0:width], e_core, SILU, bias=eb_core[:])
-            for i in range(width):
+            if j0 + width < N:
+                for i in range(width):
+                    message = work.tile([C, N], F32)
+                    nc.vector.scalar_tensor_tensor(
+                        message[:], tanh_gate[:, i, :], 1.0, silu_core[:, i, :], ADD, MULT,
+                        accum_out=twice_agg[:, j0 + i : j0 + i + 1],
+                    )
+            else:
+                nc.vector.tensor_scalar_mul(agg[:, 0:j0], twice_agg[:, 0:j0], 0.5)
+                sigmoid_gate = held.tile([C, N], F32)
+                nc.vector.tensor_scalar(sigmoid_gate[:], tanh_gate[:, 0], 0.5, 0.5, MULT, ADD)
                 message = work.tile([C, N], F32)
                 nc.vector.scalar_tensor_tensor(
-                    message[:], tanh_gate[:, i, :], 1.0, silu_core[:, i, :], ADD, MULT,
-                    accum_out=twice_agg[:, j0 + i : j0 + i + 1],
+                    message[:], sigmoid_gate[:], 1.0, silu_core[:, 0], MULT, MULT,
+                    accum_out=agg[:, j0 : j0 + 1],
                 )
             j0 += width
-
-        agg = held.tile([C, N], F32)
-        nc.vector.tensor_scalar_mul(agg[:], twice_agg[:], 0.5)
 
         nc.vector.tensor_tensor(window[:].indirect(offsets[:]), residual[:], agg[:], ADD)
         nc.sync.dma_start(out, window[:])

import concourse.mybir as mybir

F32 = mybir.dt.float32
BF16 = mybir.dt.bfloat16
U16 = mybir.dt.uint16
ADD = mybir.AluOpType.add
MULT = mybir.AluOpType.mult
TANH = mybir.ActivationFunctionType.Tanh
SILU = mybir.ActivationFunctionType.Silu

C = 128
N = 128
S = 512
JB = 4

BLOCKS = [JB] * (N // JB - 1) + [JB // 2, JB // 4, JB // 4]

FLOPS = 2 * 2 * C * (2 * C) * N


def tile_denoisingdecoder_kernel(tc, base, h, w_self, w_nbr, eb, cond, offs, out):
    nc = tc.nc
    with (
        tc.tile_pool(name="held", bufs=1) as held,
        tc.tile_pool(name="work", bufs=4) as work,
        tc.psum_pool(name="psum_e", bufs=4) as psum_e,
    ):
        h_sb = held.tile([C, N], BF16)
        w_self_sb = held.tile([C, 2 * C], BF16)
        w_nbr_sb = held.tile([C, 2 * C], BF16)
        eb_gate = held.tile([C, 1], F32)
        eb_core = held.tile([C, 1], F32)
        cond_sb = held.tile([C, 1], F32)
        offsets = held.tile([C, N // 16], U16)
        window = held.tile([C, S], F32)
        nc.sync.dma_start(w_nbr_sb[:], w_nbr)
        nc.scalar.dma_start(w_self_sb[:], w_self)
        nc.sync.dma_start(h_sb[:], h)
        nc.scalar.dma_start(eb_core[:], eb[C : 2 * C, :])
        nc.sync.dma_start(eb_gate[:], eb[0:C, :])
        nc.scalar.dma_start(cond_sb[:], cond)
        nc.sync.dma_start(offsets[:], offs)
        nc.gpsimd.dma_start(window[:], base)

        zero = held.tile([C, 1], F32)
        silu_zero = held.tile([C, 1], F32)
        nc.vector.memset(zero[:], 0.0)
        nc.scalar.activation(silu_zero[:], zero[:], SILU)

        eb_gate_half = held.tile([C, 1], F32)
        nc.vector.tensor_scalar_mul(eb_gate_half[:], eb_gate[:], 0.5)

        silu_cond = held.tile([C, 1], F32)
        nc.scalar.activation(silu_cond[:], cond_sb[:], SILU)
        residual = held.tile([C, N], F32)
        nc.vector.tensor_scalar_add(residual[:], h_sb[:], silu_cond[:])

        p = psum_e.tile([C, 2, 2 * JB], F32, tag="e_core", name="p")
        q_gate = psum_e.tile([C, N], F32, tag="e_gate", name="q_gate")
        q_core = psum_e.tile([C, N], F32, tag="e_core", name="q_core")
        early = h_sb[:, 0 : 2 * JB]
        nc.tensor.matmul(p[:, 0], w_self_sb[:, 0:C], early, start=True, stop=True)
        nc.tensor.matmul(p[:, 1], w_self_sb[:, C : 2 * C], early, start=True, stop=True)
        nc.tensor.matmul(q_gate[:], w_nbr_sb[:, 0:C], h_sb[:], start=True, stop=True)
        nc.tensor.matmul(q_core[:], w_nbr_sb[:, C : 2 * C], h_sb[:], start=True, stop=True)
        q_gate_vector = psum_e.tile([C, N], F32, tag="e_gate", name="q_gate_vector")
        q_core_vector = psum_e.tile([C, N], F32, tag="e_core", name="q_core_vector")
        nc.tensor.matmul(q_gate_vector[:], w_nbr_sb[:, 0:C], h_sb[:], start=True, stop=True)
        nc.tensor.matmul(q_core_vector[:], w_nbr_sb[:, C : 2 * C], h_sb[:], start=True, stop=True)
        p_gate_half = held.tile([C, 2 * JB], F32)
        p_core = held.tile([C, 2 * JB], F32)
        nc.vector.tensor_scalar(p_gate_half[:], p[:, 0], eb_gate[:], 0.5, ADD, MULT)
        nc.vector.tensor_scalar_add(p_core[:], p[:, 1], eb_core[:])
        half_e_gate = held.tile([C, JB, N], F32)
        sbuf_e_core = held.tile([C, JB, N], F32)
        for e, q, scale, p_eb in (
            (half_e_gate, q_gate_vector, 0.5, p_gate_half),
            (sbuf_e_core, q_core_vector, 1.0, p_core),
        ):
            nc.vector.scalar_tensor_tensor(
                e[:],
                q[:].unsqueeze(1).to_broadcast([C, JB, N]),
                scale,
                p_eb[:, JB : 2 * JB].unsqueeze(2).to_broadcast([C, JB, N]),
                MULT,
                ADD,
            )

        twice_agg = held.tile([C, N], F32)
        agg = held.tile([C, N], F32)
        j0 = 0
        for width in BLOCKS:
            tanh_gate = work.tile([C, JB, N], F32)
            silu_core = work.tile([C, JB, N], F32)
            if j0 == 0:
                for j in range(width):
                    nc.scalar.activation(
                        tanh_gate[:, j], q_gate[:], TANH, bias=p_gate_half[:, j : j + 1], scale=0.5
                    )
                    nc.scalar.activation(
                        silu_core[:, j], q_core[:], SILU, bias=p_core[:, j : j + 1]
                    )
            elif j0 == JB:
                nc.scalar.activation(tanh_gate[:], half_e_gate[:], TANH)
                nc.scalar.activation(silu_core[:], sbuf_e_core[:], SILU)
            else:
                sending = h_sb[:].unsqueeze(1).to_broadcast([C, width, N])
                receiving = h_sb[:, j0 : j0 + width].unsqueeze(2).to_broadcast([C, width, N])
                gate_tile = psum_e.tile([C, JB, N], F32, tag="e_gate", name="gate_tile")
                core_tile = psum_e.tile([C, JB, N], F32, tag="e_core", name="core_tile")
                e_gate, e_core = gate_tile[:, 0:width], core_tile[:, 0:width]
                nc.tensor.matmul(e_gate, w_self_sb[:, 0:C], receiving, start=True, stop=False)
                nc.tensor.matmul(e_gate, w_nbr_sb[:, 0:C], sending, start=False, stop=True)
                nc.tensor.matmul(e_core, w_self_sb[:, C : 2 * C], receiving, start=True, stop=False)
                nc.tensor.matmul(e_core, w_nbr_sb[:, C : 2 * C], sending, start=False, stop=True)
                nc.scalar.activation(
                    tanh_gate[:, 0:width], e_gate, TANH, bias=eb_gate_half[:], scale=0.5
                )
                nc.scalar.activation(silu_core[:, 0:width], e_core, SILU, bias=eb_core[:])
            if j0 + width < N:
                for i in range(width):
                    message = work.tile([C, N], F32)
                    nc.vector.scalar_tensor_tensor(
                        message[:], tanh_gate[:, i, :], 1.0, silu_core[:, i, :], ADD, MULT,
                        accum_out=twice_agg[:, j0 + i : j0 + i + 1],
                    )
            else:
                nc.vector.tensor_scalar_mul(agg[:, 0:j0], twice_agg[:, 0:j0], 0.5)
                sigmoid_gate = held.tile([C, N], F32)
                nc.vector.tensor_scalar(sigmoid_gate[:], tanh_gate[:, 0], 0.5, 0.5, MULT, ADD)
                message = work.tile([C, N], F32)
                nc.vector.scalar_tensor_tensor(
                    message[:], sigmoid_gate[:], 1.0, silu_core[:, 0], MULT, MULT,
                    accum_out=agg[:, j0 : j0 + 1],
                )
            j0 += width

        nc.vector.tensor_tensor(window[:].indirect(offsets[:]), residual[:], agg[:], ADD)
        nc.sync.dma_start(out, window[:])
